import numpy as np
import ml_dtypes


def mxq(x, axis, fmt="e4m3"):
    dtype, down = {"e4m3": (ml_dtypes.float8_e4m3fn, 7), "e5m2": (ml_dtypes.float8_e5m2, 14)}[fmt]
    v = np.moveaxis(np.asarray(x, np.float32).astype(ml_dtypes.bfloat16).astype(np.float64), axis, -1)
    blocks = v.reshape(v.shape[:-1] + (-1, 32))
    amax = np.abs(blocks).max(-1, keepdims=True)
    byte = np.maximum(np.where(amax > 0, np.frexp(amax)[1] - 1 + 127, 0) - down, 1)
    scale = np.exp2(byte - 127.0)
    codes = (blocks / scale).astype(np.float32).astype(dtype).astype(np.float64)
    return np.moveaxis((codes * scale).reshape(v.shape), -1, axis)


WIDE = False


def mx_kscale(k):
    if not WIDE:
        return np.ones(k)
    levels = np.array([10, -10, 5, -5, 0])
    a = np.random.permutation(np.resize(levels, k // 512 * 4)).reshape(k // 512, 4)
    idx = np.arange(k)
    return np.exp2(a[idx // 512, idx % 128 // 32])


BF16 = ml_dtypes.bfloat16


def bf(x):
    return np.asarray(x, np.float32).astype(BF16)


def f64(x):
    return np.asarray(x).astype(np.float64)


B, IN, H = 4096, 512, 512


def sigmoid(v):
    return 1.0 / (1.0 + np.exp(-v))


def setup_inputs():
    s, t = mx_kscale(IN), mx_kscale(H)
    a = np.sqrt(2.0 / (IN + H))
    return {
        "x": bf(np.random.standard_normal((B, IN)) * s),
        "h_prev": bf(np.random.standard_normal((B, H)) * t),
        "m_prev": bf(np.random.standard_normal((B, H)) * 0.5),
        "Wi_x": bf(np.random.standard_normal((H, IN)) * a / s),
        "b_i": bf(np.random.standard_normal(H) * 0.3),
        "Wi_h": bf(np.random.standard_normal((H, H)) * a / t),
        "Wf_x": bf(np.random.standard_normal((H, IN)) * a / s),
        "b_f": bf(2.0 + np.random.standard_normal(H) * 0.3),
        "Wf_h": bf(np.random.standard_normal((H, H)) * a / t),
    }


def reference(x, h_prev, m_prev, Wi_x, b_i, Wi_h, Wf_x, b_f, Wf_h):
    xq = mxq(f64(x), 1, "e4m3")
    hq = mxq(f64(h_prev), 1, "e4m3")
    i_tilde = (xq @ mxq(f64(Wi_x), 1, "e4m3").T) + f64(b_i) + (hq @ mxq(f64(Wi_h), 1, "e4m3").T)
    f_aff = (xq @ mxq(f64(Wf_x), 1, "e4m3").T) + f64(b_f) + (hq @ mxq(f64(Wf_h), 1, "e4m3").T)
    log_f = np.log(np.maximum(sigmoid(f_aff), 1e-8))
    m_t = np.maximum(log_f + f64(m_prev), i_tilde)
    i_prime = np.exp(i_tilde - m_t)
    f_prime = np.exp(log_f + f64(m_prev) - m_t)
    return m_t, i_prime, f_prime

@@ -1,0 +1,291 @@
+from contextlib import ExitStack
+
+import concourse.mybir as mybir
+from concourse.masks import make_identity
+
+F32 = mybir.dt.float32
+BF16 = mybir.dt.bfloat16
+U32 = mybir.dt.uint32
+U8 = mybir.dt.uint8
+FP8X4 = mybir.dt.float8_e4m3fn_x4
+ACT = mybir.ActivationFunctionType
+ALU = mybir.AluOpType
+
+P = 128
+BATCH = 4096
+FEAT = 512
+HID = 512
+WORDS = FEAT // 2
+CHUNKS = HID // P
+
+PAIR_TILES = 2
+PAIR_ROWS = PAIR_TILES * P
+GROUP_PAIRS = 2
+GROUP_TILES = GROUP_PAIRS * PAIR_TILES
+GROUP_ROWS = GROUP_TILES * P
+ROUND_PAIRS = 4
+ROUND_GROUPS = ROUND_PAIRS // GROUP_PAIRS
+N_PAIRS = BATCH // PAIR_ROWS
+N_GROUPS = BATCH // GROUP_ROWS
+
+LEAD_LOG = 2
+LEAD_QUANTISE = LEAD_LOG + ROUND_PAIRS + 1
+LEAD_TRANSPOSE = LEAD_QUANTISE + 1
+LEAD_M = 6
+LAG_EXP = 2
+LOAD_AHEAD_GROUPS = 2
+
+E_MAX = 1.0e8 - 1.0
+
+FLOPS = 2 * BATCH * HID * FEAT * 4
+
+
+def tile_slstmlayer_pa_t_kernel(
+    tc, x, h_prev, m_prev, Wi_x, b_i, Wi_h, Wf_x, b_f, Wf_h, out_0, out_1, out_2
+):
+    nc = tc.nc
+    with ExitStack() as ctx:
+        consts = ctx.enter_context(tc.tile_pool(name="consts", bufs=1))
+        raws = ctx.enter_context(tc.tile_pool(name="raws", bufs=8))
+        m_pool = ctx.enter_context(tc.tile_pool(name="m_pool", bufs=4))
+        grouped_pool = ctx.enter_context(tc.tile_pool(name="grouped_pool", bufs=3))
+        codes_pool = ctx.enter_context(tc.tile_pool(name="codes_pool", bufs=N_GROUPS))
+        e_pool = ctx.enter_context(tc.tile_pool(name="e_pool", bufs=5))
+        short_pool = ctx.enter_context(tc.tile_pool(name="short_pool", bufs=3))
+        long_pool = ctx.enter_context(tc.tile_pool(name="long_pool", bufs=5))
+        psum = ctx.enter_context(tc.psum_pool(name="psum", bufs=2))
+        ctx.enter_context(tc.manual_schedule())
+
+        ident_f32 = consts.tile([P, P], F32, tag="ident_f32")
+        make_identity(nc, ident_f32[:])
+        ident_bf16 = consts.tile([P, P], BF16, tag="ident_bf16")
+        make_identity(nc, ident_bf16[:])
+        one = consts.tile([P, 1], F32, tag="one")
+        nc.vector.memset(one[:], 1.0)
+        warm = consts.tile([P, 1], F32, tag="warm")
+        nc.scalar.activation(out=warm[:], in_=one[:], func=ACT.Exp)
+
+        def group_rows(dram, g):
+            rows = dram[g * GROUP_ROWS : (g + 1) * GROUP_ROWS, :]
+            return rows.rearrange("(p j) k -> p (j k)", j=GROUP_TILES)
+
+        def pair_rows(dram, s):
+            g, half = divmod(s, GROUP_PAIRS)
+            rows = dram[g * GROUP_ROWS : (g + 1) * GROUP_ROWS, :]
+            return rows.rearrange("(p a t) k -> a p (t k)", a=GROUP_PAIRS, t=PAIR_TILES)[half]
+
+        def load_activation(dram, g):
+            raw = raws.tile([P, GROUP_TILES * FEAT], BF16, tag="raw")
+            nc.sync.dma_start(out=raw[:], in_=group_rows(dram, g))
+            return raw
+
+        def load_weight(w):
+            raw = raws.tile([P, GROUP_TILES * FEAT], BF16, tag="raw")
+            nc.sync.dma_start(
+                out=raw[:].rearrange("p (c k) -> p c k", c=CHUNKS),
+                in_=w.rearrange("(c p) k -> p c k", p=P),
+            )
+            return raw
+
+        def new_operand(raw, pool, name, grouped_tag):
+            codes = pool.tile([P, GROUP_ROWS], U32, tag=name + "_codes", align_bytes=64)
+            scales = pool.tile([P, GROUP_ROWS], U8, tag=name + "_scales", align_bytes=64)
+            return {"raw": raw, "codes": codes, "scales": scales, "grouped_tag": grouped_tag, "grouped": {}}
+
+        def transpose_half(operand, half):
+            words = operand["raw"][:].bitcast(F32)
+            bank = psum.tile([P, 2, PAIR_ROWS], F32, tag="tr")
+            for t in range(PAIR_TILES):
+                for u in range(2):
+                    first = (half * PAIR_TILES + t) * WORDS + u * P
+                    nc.tensor.transpose(
+                        bank[:, u, t * P : (t + 1) * P], words[:, first : first + P], ident_f32[:]
+                    )
+            return bank
+
+        def copy_out_half(operand, half, bank, copy):
+            grouped = grouped_pool.tile([P, 4 * PAIR_ROWS], BF16, tag=operand["grouped_tag"], align_bytes=64)
+            copy(
+                out=grouped[:].bitcast(F32).rearrange("p (r u) -> p r u", u=2),
+                in_=bank[:].rearrange("p u r -> p r u"),
+            )
+            operand["grouped"][half] = grouped
+
+        def quantise_half(operand, half):
+            rows = slice(half * PAIR_ROWS, (half + 1) * PAIR_ROWS)
+            nc.vector.quantize_mx(
+                out=operand["codes"][:, rows].bitcast(FP8X4),
+                scales=operand["scales"][:, rows],
+                in_=operand["grouped"][half][:],
+            )
+
+        def prepare_weight(raw, name, second_copy):
+            operand = new_operand(raw, consts, name, "w_grouped")
+            copy_out_half(operand, 0, transpose_half(operand, 0), nc.vector.tensor_copy)
+            copy_out_half(operand, 1, transpose_half(operand, 1), second_copy)
+            quantise_half(operand, 0)
+            quantise_half(operand, 1)
+            return operand
+
+        def mx_product(out, stationary, stationary_cols, moving, start, stop):
+            nc.tensor.matmul_mx(
+                out=out,
+                lhsT=stationary["codes"][:, stationary_cols].bitcast(FP8X4),
+                lhsT_scale=stationary["scales"][:, stationary_cols],
+                rhs=moving["codes"][:].bitcast(FP8X4),
+                rhs_scale=moving["scales"][:],
+                start=start,
+                stop=stop,
+            )
+
+        bias_rows = consts.tile([P, P], BF16, tag="bias_rows")
+        nc.vector.memset(bias_rows[:], 0.0)
+        nc.scalar.dma_start(out=bias_rows[0:CHUNKS, :], in_=b_f.rearrange("(c p) -> c p", p=P))
+
+        wfx_raw = load_weight(Wf_x)
+        wfh_raw = load_weight(Wf_h)
+        x_raw = {}
+        h_raw = {}
+        for g in range(LOAD_AHEAD_GROUPS):
+            x_raw[g] = load_activation(x, g)
+            h_raw[g] = load_activation(h_prev, g)
+        bi_all = consts.tile([P, HID], BF16, tag="bi_all")
+        nc.sync.dma_start(out=bi_all[:], in_=b_i.partition_broadcast(P))
+
+        bias_bank = psum.tile([P, P], BF16, tag="tr")
+        nc.tensor.transpose(bias_bank[:], bias_rows[:], ident_bf16[:])
+        neg_bf = consts.tile([P, CHUNKS], F32, tag="neg_bf")
+        nc.vector.tensor_scalar(
+            out=neg_bf[:], in0=bias_bank[:, 0:CHUNKS], scalar1=-1.0, scalar2=None, op0=ALU.mult
+        )
+
+        weights = {}
+        weights["fx"] = prepare_weight(wfx_raw, "wfx", nc.scalar.copy)
+        weights["fh"] = prepare_weight(wfh_raw, "wfh", nc.scalar.copy)
+
+        x_ops = {}
+        h_ops = {}
+        m_rows = {}
+        e_tiles = {}
+        i_args = {}
+        f_args = {}
+        unclamped = None
+
+        for s in range(-LEAD_TRANSPOSE, N_PAIRS + LAG_EXP):
+            pair_t = s + LEAD_TRANSPOSE
+            pair_q = s + LEAD_QUANTISE
+            pair_l = s + LEAD_LOG
+            pair_e = s - LAG_EXP
+            transposing = pair_t < N_PAIRS
+            quantising = 0 <= pair_q < N_PAIRS
+            coming, k = divmod(pair_l, ROUND_PAIRS)
+            g_f = (coming + 1) * ROUND_GROUPS + k - 2
+            forgetting = k >= 2 and 0 <= g_f < N_GROUPS
+            chain = 0 <= s < N_PAIRS
+
+            if pair_t % GROUP_PAIRS == 0:
+                g_load = pair_t // GROUP_PAIRS + LOAD_AHEAD_GROUPS
+                if g_load < N_GROUPS:
+                    x_raw[g_load] = load_activation(x, g_load)
+                    h_raw[g_load] = load_activation(h_prev, g_load)
+            if (s + LEAD_M) % GROUP_PAIRS == 0 and 0 <= s + LEAD_M < N_PAIRS:
+                m_tile = m_pool.tile([P, GROUP_TILES * HID], BF16, tag="m")
+                nc.sync.dma_start(out=m_tile[:], in_=group_rows(m_prev, (s + LEAD_M) // GROUP_PAIRS))
+                m_rows[(s + LEAD_M) // GROUP_PAIRS] = m_tile
+
+            if s == -LEAD_LOG - 3:
+                wix_raw = load_weight(Wi_x)
+                wih_raw = load_weight(Wi_h)
+
+            if unclamped is not None:
+                flat = e_tiles[unclamped][:].rearrange("p c b -> p (c b)")
+                nc.gpsimd.tensor_scalar(out=flat, in0=flat, scalar1=E_MAX, scalar2=0.0, op0=ALU.min, op1=ALU.max)
+                unclamped = None
+
+            if k == 0 and 0 <= pair_l < N_PAIRS:
+                for g in range(coming * ROUND_GROUPS, (coming + 1) * ROUND_GROUPS):
+                    flat = e_tiles[g][:].rearrange("p c b -> p (c b)")
+                    nc.scalar.activation(out=flat, in_=flat, func=ACT.Ln, bias=one[:], scale=1.0)
+
+            if chain:
+                g_s, half_s = divmod(s, GROUP_PAIRS)
+                logf_banks = []
+                for t in range(PAIR_TILES):
+                    j = half_s * PAIR_TILES + t
+                    logf_bank = psum.tile([P, HID], F32, tag="lb")
+                    for c in range(CHUNKS):
+                        nc.tensor.transpose(
+                            logf_bank[:, c * P : (c + 1) * P],
+                            e_tiles[g_s][:, c, j * P : (j + 1) * P],
+                            ident_f32[:],
+                        )
+                    logf_banks.append(logf_bank)
+                i_banks = []
+                for t in range(PAIR_TILES):
+                    j = half_s * PAIR_TILES + t
+                    i_bank = psum.tile([P, HID], F32, tag="pi")
+                    tile_cols = slice(j * P, (j + 1) * P)
+                    mx_product(i_bank[:], x_ops[g_s], tile_cols, weights["ix"], True, False)
+                    mx_product(i_bank[:], h_ops[g_s], tile_cols, weights["ih"], False, True)
+                    i_banks.append(i_bank)
+
+            if forgetting:
+                e_tile = e_pool.tile([P, CHUNKS, GROUP_ROWS], F32, tag="e")
+                e_tiles[g_f] = e_tile
+                for c in range(CHUNKS):
+                    f_bank = psum.tile([P, GROUP_ROWS], F32, tag="pf")
+                    chunk_cols = slice(c * P, (c + 1) * P)
+                    mx_product(f_bank[:], weights["fx"], chunk_cols, x_ops[g_f], True, False)
+                    mx_product(f_bank[:], weights["fh"], chunk_cols, h_ops[g_f], False, True)
+                    nc.scalar.activation(
+                        out=e_tiles[g_f][:, c, :], in_=f_bank[:], func=ACT.Exp,
+                        bias=neg_bf[:, c : c + 1], scale=-1.0,
+                    )
+                unclamped = g_f
+
+            if chain:
+                i_tilde = short_pool.tile([P, PAIR_TILES * HID], F32, tag="i_tilde", bufs=2)
+                f_arg = long_pool.tile([P, PAIR_TILES * HID], F32, tag="f_arg")
+                m_t = short_pool.tile([P, PAIR_TILES * HID], F32, tag="m_t")
+                i_arg = long_pool.tile([P, PAIR_TILES * HID], F32, tag="i_arg")
+                for t in range(PAIR_TILES):
+                    j = half_s * PAIR_TILES + t
+                    cols = slice(t * HID, (t + 1) * HID)
+                    nc.vector.tensor_tensor(out=i_tilde[:, cols], in0=i_banks[t][:], in1=bi_all[:], op=ALU.add)
+                    nc.vector.scalar_tensor_tensor(
+                        out=f_arg[:, cols], in0=logf_banks[t][:], scalar=-1.0,
+                        in1=m_rows[g_s][:, j * HID : (j + 1) * HID], op0=ALU.mult, op1=ALU.add,
+                    )
+            if chain:
+                nc.vector.tensor_tensor(out=m_t[:], in0=f_arg[:], in1=i_tilde[:], op=ALU.max)
+            if quantising:
+                quantise_half(x_ops[pair_q // GROUP_PAIRS], pair_q % GROUP_PAIRS)
+            if chain:
+                nc.vector.tensor_tensor(out=i_arg[:], in0=i_tilde[:], in1=m_t[:], op=ALU.subtract)
+            if quantising:
+                quantise_half(h_ops[pair_q // GROUP_PAIRS], pair_q % GROUP_PAIRS)
+            if chain:
+                nc.gpsimd.tensor_tensor(out=f_arg[:], in0=f_arg[:], in1=m_t[:], op=ALU.subtract)
+                nc.sync.dma_start(out=pair_rows(out_0, s), in_=m_t[:])
+                i_args[s] = i_arg
+                f_args[s] = f_arg
+
+            if 0 <= pair_e < N_PAIRS:
+                nc.scalar.activation(out=i_args[pair_e][:], in_=i_args[pair_e][:], func=ACT.Exp)
+                nc.sync.dma_start(out=pair_rows(out_1, pair_e), in_=i_args[pair_e][:])
+                nc.scalar.activation(out=f_args[pair_e][:], in_=f_args[pair_e][:], func=ACT.Exp)
+                nc.sync.dma_start(out=pair_rows(out_2, pair_e), in_=f_args[pair_e][:])
+
+            if transposing:
+                g_t, half_t = divmod(pair_t, GROUP_PAIRS)
+                if half_t == 0:
+                    x_ops[g_t] = new_operand(x_raw[g_t], codes_pool, "x", "x_grouped")
+                    h_ops[g_t] = new_operand(h_raw[g_t], codes_pool, "h", "h_grouped")
+                x_bank = transpose_half(x_ops[g_t], half_t)
+                h_bank = transpose_half(h_ops[g_t], half_t)
+                copy_out_half(x_ops[g_t], half_t, x_bank, nc.vector.tensor_copy)
+                copy_out_half(h_ops[g_t], half_t, h_bank, nc.vector.tensor_copy if k == 0 else nc.scalar.copy)
+
+            if s == -LEAD_LOG:
+                weights["ix"] = prepare_weight(wix_raw, "wix", nc.vector.tensor_copy)
+                weights["ih"] = prepare_weight(wih_raw, "wih", nc.vector.tensor_copy)

@@ -167,6 +167,8 @@ def tile_slstmlayer_pa_t_kernel(
         h_ops = {}
         m_rows = {}
         e_tiles = {}
+        i_tildes = {}
+        m_ts = {}
         i_args = {}
         f_args = {}
         unclamped = None
@@ -196,11 +198,6 @@ def tile_slstmlayer_pa_t_kernel(
             if s == -LEAD_LOG - 3:
                 wix_raw = load_weight(Wi_x)
                 wih_raw = load_weight(Wi_h)
-
-            if unclamped is not None:
-                flat = e_tiles[unclamped][:].rearrange("p c b -> p (c b)")
-                nc.gpsimd.tensor_scalar(out=flat, in0=flat, scalar1=E_MAX, scalar2=0.0, op0=ALU.min, op1=ALU.max)
-                unclamped = None
 
             if k == 0 and 0 <= pair_l < N_PAIRS:
                 for g in range(coming * ROUND_GROUPS, (coming + 1) * ROUND_GROUPS):
@@ -244,10 +241,9 @@ def tile_slstmlayer_pa_t_kernel(
                 unclamped = g_f
 
             if chain:
-                i_tilde = short_pool.tile([P, PAIR_TILES * HID], F32, tag="i_tilde", bufs=2)
+                i_tilde = short_pool.tile([P, PAIR_TILES * HID], F32, tag="i_tilde")
                 f_arg = long_pool.tile([P, PAIR_TILES * HID], F32, tag="f_arg")
                 m_t = short_pool.tile([P, PAIR_TILES * HID], F32, tag="m_t")
-                i_arg = long_pool.tile([P, PAIR_TILES * HID], F32, tag="i_arg")
                 for t in range(PAIR_TILES):
                     j = half_s * PAIR_TILES + t
                     cols = slice(t * HID, (t + 1) * HID)
@@ -256,18 +252,24 @@ def tile_slstmlayer_pa_t_kernel(
                         out=f_arg[:, cols], in0=logf_banks[t][:], scalar=-1.0,
                         in1=m_rows[g_s][:, j * HID : (j + 1) * HID], op0=ALU.mult, op1=ALU.add,
                     )
-            if chain:
-                nc.vector.tensor_tensor(out=m_t[:], in0=f_arg[:], in1=i_tilde[:], op=ALU.max)
+            if 0 <= s - 1 < N_PAIRS:
+                i_arg = long_pool.tile([P, PAIR_TILES * HID], F32, tag="i_arg")
+                nc.vector.tensor_tensor(out=i_arg[:], in0=i_tildes[s - 1][:], in1=m_ts[s - 1][:], op=ALU.subtract)
+                i_args[s - 1] = i_arg
             if quantising:
                 quantise_half(x_ops[pair_q // GROUP_PAIRS], pair_q % GROUP_PAIRS)
-            if chain:
-                nc.vector.tensor_tensor(out=i_arg[:], in0=i_tilde[:], in1=m_t[:], op=ALU.subtract)
             if quantising:
                 quantise_half(h_ops[pair_q // GROUP_PAIRS], pair_q % GROUP_PAIRS)
+            if unclamped is not None:
+                flat = e_tiles[unclamped][:].rearrange("p c b -> p (c b)")
+                nc.vector.tensor_scalar_min(out=flat, in0=flat, scalar1=E_MAX)
+                unclamped = None
             if chain:
+                nc.vector.tensor_tensor(out=m_t[:], in0=f_arg[:], in1=i_tilde[:], op=ALU.max)
                 nc.gpsimd.tensor_tensor(out=f_arg[:], in0=f_arg[:], in1=m_t[:], op=ALU.subtract)
                 nc.sync.dma_start(out=pair_rows(out_0, s), in_=m_t[:])
-                i_args[s] = i_arg
+                i_tildes[s] = i_tilde
+                m_ts[s] = m_t
                 f_args[s] = f_arg
 
             if 0 <= pair_e < N_PAIRS:
@@ -283,8 +285,9 @@ def tile_slstmlayer_pa_t_kernel(
                     h_ops[g_t] = new_operand(h_raw[g_t], codes_pool, "h", "h_grouped")
                 x_bank = transpose_half(x_ops[g_t], half_t)
                 h_bank = transpose_half(h_ops[g_t], half_t)
-                copy_out_half(x_ops[g_t], half_t, x_bank, nc.vector.tensor_copy)
-                copy_out_half(h_ops[g_t], half_t, h_bank, nc.vector.tensor_copy if k == 0 else nc.scalar.copy)
+                copy = nc.vector.tensor_copy if k == 0 else nc.scalar.copy
+                copy_out_half(x_ops[g_t], half_t, x_bank, copy)
+                copy_out_half(h_ops[g_t], half_t, h_bank, copy)
 
             if s == -LEAD_LOG:
                 weights["ix"] = prepare_weight(wix_raw, "wix", nc.vector.tensor_copy)

@@ -23,19 +23,14 @@ PAIR_ROWS = PAIR_TILES * P
 GROUP_PAIRS = 2
 GROUP_TILES = GROUP_PAIRS * PAIR_TILES
 GROUP_ROWS = GROUP_TILES * P
-ROUND_PAIRS = 4
-ROUND_GROUPS = ROUND_PAIRS // GROUP_PAIRS
-N_PAIRS = BATCH // PAIR_ROWS
+ROUND_GROUPS = 2
+ROUND_PAIRS = ROUND_GROUPS * GROUP_PAIRS
 N_GROUPS = BATCH // GROUP_ROWS
+N_ROUNDS = N_GROUPS // ROUND_GROUPS
+N_PAIRS = BATCH // PAIR_ROWS
+LEAD_PAIRS = 2 * ROUND_PAIRS
 
-LEAD_LOG = 2
-LEAD_QUANTISE = LEAD_LOG + ROUND_PAIRS + 1
-LEAD_TRANSPOSE = LEAD_QUANTISE + 1
-LEAD_M = 6
-LAG_EXP = 2
-LOAD_AHEAD_GROUPS = 2
-
-E_MAX = 1.0e8 - 1.0
+SIGMOID_MIN = 1.0e-8
 
 FLOPS = 2 * BATCH * HID * FEAT * 4
 
@@ -46,13 +41,13 @@ def tile_slstmlayer_pa_t_kernel(
     nc = tc.nc
     with ExitStack() as ctx:
         consts = ctx.enter_context(tc.tile_pool(name="consts", bufs=1))
-        raws = ctx.enter_context(tc.tile_pool(name="raws", bufs=8))
-        m_pool = ctx.enter_context(tc.tile_pool(name="m_pool", bufs=4))
+        raws = ctx.enter_context(tc.tile_pool(name="raws", bufs=4 * ROUND_GROUPS))
+        m_pool = ctx.enter_context(tc.tile_pool(name="m_pool", bufs=2 * ROUND_GROUPS))
         grouped_pool = ctx.enter_context(tc.tile_pool(name="grouped_pool", bufs=3))
-        codes_pool = ctx.enter_context(tc.tile_pool(name="codes_pool", bufs=N_GROUPS))
-        e_pool = ctx.enter_context(tc.tile_pool(name="e_pool", bufs=5))
-        short_pool = ctx.enter_context(tc.tile_pool(name="short_pool", bufs=3))
-        long_pool = ctx.enter_context(tc.tile_pool(name="long_pool", bufs=5))
+        codes_pool = ctx.enter_context(tc.tile_pool(name="codes_pool", bufs=3 * ROUND_GROUPS))
+        gate_pool = ctx.enter_context(tc.tile_pool(name="gate_pool", bufs=2 * ROUND_GROUPS))
+        arg_pool = ctx.enter_context(tc.tile_pool(name="arg_pool", bufs=ROUND_PAIRS + 3))
+        m_t_pool = ctx.enter_context(tc.tile_pool(name="m_t_pool", bufs=3))
         psum = ctx.enter_context(tc.psum_pool(name="psum", bufs=2))
         ctx.enter_context(tc.manual_schedule())
 
@@ -60,41 +55,56 @@ def tile_slstmlayer_pa_t_kernel(
         make_identity(nc, ident_f32[:])
         ident_bf16 = consts.tile([P, P], BF16, tag="ident_bf16")
         make_identity(nc, ident_bf16[:])
-        one = consts.tile([P, 1], F32, tag="one")
-        nc.vector.memset(one[:], 1.0)
-        warm = consts.tile([P, 1], F32, tag="warm")
-        nc.scalar.activation(out=warm[:], in_=one[:], func=ACT.Exp)
-
-        def group_rows(dram, g):
-            rows = dram[g * GROUP_ROWS : (g + 1) * GROUP_ROWS, :]
-            return rows.rearrange("(p j) k -> p (j k)", j=GROUP_TILES)
 
         def pair_rows(dram, s):
-            g, half = divmod(s, GROUP_PAIRS)
-            rows = dram[g * GROUP_ROWS : (g + 1) * GROUP_ROWS, :]
-            return rows.rearrange("(p a t) k -> a p (t k)", a=GROUP_PAIRS, t=PAIR_TILES)[half]
+            rows = dram[s * PAIR_ROWS : (s + 1) * PAIR_ROWS, :]
+            return rows.rearrange("(p t) k -> p (t k)", t=PAIR_TILES)
 
-        def load_activation(dram, g):
-            raw = raws.tile([P, GROUP_TILES * FEAT], BF16, tag="raw")
-            nc.sync.dma_start(out=raw[:], in_=group_rows(dram, g))
-            return raw
+        def load_group(rows_tile, dram, g):
+            rows = dram[g * GROUP_ROWS : (g + 1) * GROUP_ROWS, :]
+            nc.sync.dma_start(
+                out=rows_tile[:].rearrange("p (a w) -> p a w", a=GROUP_PAIRS),
+                in_=rows.rearrange("(a p t) k -> p a (t k)", a=GROUP_PAIRS, t=PAIR_TILES),
+            )
 
         def load_weight(w):
-            raw = raws.tile([P, GROUP_TILES * FEAT], BF16, tag="raw")
+            raw = raws.tile([P, GROUP_TILES * FEAT], BF16, tag="w_raw", bufs=2)
             nc.sync.dma_start(
                 out=raw[:].rearrange("p (c k) -> p c k", c=CHUNKS),
                 in_=w.rearrange("(c p) k -> p c k", p=P),
             )
             return raw
 
+        x_raw = {}
+        h_raw = {}
+        m_rows = {}
+
+        def round_groups(k):
+            return range(k * ROUND_GROUPS, (k + 1) * ROUND_GROUPS) if k < N_ROUNDS else ()
+
+        def group_pairs(g):
+            return range(g * GROUP_PAIRS, (g + 1) * GROUP_PAIRS)
+
+        def load_activations(k):
+            for g in round_groups(k):
+                x_raw[g] = raws.tile([P, GROUP_TILES * FEAT], BF16, tag="raw", name="x_raw")
+                load_group(x_raw[g], x, g)
+                h_raw[g] = raws.tile([P, GROUP_TILES * FEAT], BF16, tag="raw", name="h_raw")
+                load_group(h_raw[g], h_prev, g)
+
+        def load_m_prev(k):
+            for g in round_groups(k):
+                m_rows[g] = m_pool.tile([P, GROUP_TILES * HID], BF16, tag="m", name="m_rows")
+                load_group(m_rows[g], m_prev, g)
+
         def new_operand(raw, pool, name, grouped_tag):
             codes = pool.tile([P, GROUP_ROWS], U32, tag=name + "_codes", align_bytes=64)
             scales = pool.tile([P, GROUP_ROWS], U8, tag=name + "_scales", align_bytes=64)
             return {"raw": raw, "codes": codes, "scales": scales, "grouped_tag": grouped_tag, "grouped": {}}
 
-        def transpose_half(operand, half):
+        def transpose_half(operand, half, bank_tag):
             words = operand["raw"][:].bitcast(F32)
-            bank = psum.tile([P, 2, PAIR_ROWS], F32, tag="tr")
+            bank = psum.tile([P, 2, PAIR_ROWS], F32, tag=bank_tag)
             for t in range(PAIR_TILES):
                 for u in range(2):
                     first = (half * PAIR_TILES + t) * WORDS + u * P
@@ -121,8 +131,8 @@ def tile_slstmlayer_pa_t_kernel(
 
         def prepare_weight(raw, name, second_copy):
             operand = new_operand(raw, consts, name, "w_grouped")
-            copy_out_half(operand, 0, transpose_half(operand, 0), nc.vector.tensor_copy)
-            copy_out_half(operand, 1, transpose_half(operand, 1), second_copy)
+            copy_out_half(operand, 0, transpose_half(operand, 0, "pi"), nc.vector.tensor_copy)
+            copy_out_half(operand, 1, transpose_half(operand, 1, "pi"), second_copy)
             quantise_half(operand, 0)
             quantise_half(operand, 1)
             return operand
@@ -138,157 +148,169 @@ def tile_slstmlayer_pa_t_kernel(
                 stop=stop,
             )
 
+        weights = {}
+        x_ops = {}
+        h_ops = {}
+        gates = {}
+        word_banks = {}
+        banks = {}
+        i_args = {}
+        f_args = {}
+
+        def forget_gate(g):
+            gates[g] = gate_pool.tile([P, CHUNKS, GROUP_ROWS], F32, tag="gate", name="gate")
+            for c in range(CHUNKS):
+                f_bank = psum.tile([P, GROUP_ROWS], F32, tag="pf")
+                chunk_cols = slice(c * P, (c + 1) * P)
+                mx_product(f_bank[:], weights["fx"], chunk_cols, x_ops[g], True, False)
+                mx_product(f_bank[:], weights["fh"], chunk_cols, h_ops[g], False, True)
+                nc.scalar.activation(
+                    out=gates[g][:, c, :], in_=f_bank[:], func=ACT.Sigmoid,
+                    bias=bf_col[:, c : c + 1], scale=1.0,
+                )
+                nc.gpsimd.tensor_scalar(
+                    out=gates[g][:, c, :], in0=gates[g][:, c, :],
+                    scalar1=1.0, scalar2=SIGMOID_MIN, op0=ALU.min, op1=ALU.max,
+                )
+
+        def logarithms(k):
+            for g in round_groups(k):
+                flat = gates[g][:].rearrange("p c b -> p (c b)")
+                nc.scalar.activation(out=flat, in_=flat, func=ACT.Ln)
+
+        def transpose_pair(q):
+            if q < N_PAIRS:
+                g, half = divmod(q, GROUP_PAIRS)
+                if half == 0:
+                    x_ops[g] = new_operand(x_raw[g], codes_pool, "x", "x_grouped")
+                    h_ops[g] = new_operand(h_raw[g], codes_pool, "h", "h_grouped")
+                word_banks[q] = (transpose_half(x_ops[g], half, "tr"), transpose_half(h_ops[g], half, "tr"))
+
+        def copy_out_pair(q):
+            if q < N_PAIRS:
+                g, half = divmod(q, GROUP_PAIRS)
+                x_bank, h_bank = word_banks[q]
+                copy_out_half(x_ops[g], half, x_bank, nc.vector.tensor_copy)
+                copy_out_half(h_ops[g], half, h_bank, nc.vector.tensor_copy)
+
+        def quantise_pair(q):
+            if q < N_PAIRS:
+                g, half = divmod(q, GROUP_PAIRS)
+                quantise_half(x_ops[g], half)
+                quantise_half(h_ops[g], half)
+
+        def chain_banks(s):
+            g, half = divmod(s, GROUP_PAIRS)
+            i_banks = []
+            for t in range(PAIR_TILES):
+                j = half * PAIR_TILES + t
+                i_bank = psum.tile([P, HID], F32, tag="pi")
+                tile_cols = slice(j * P, (j + 1) * P)
+                mx_product(i_bank[:], x_ops[g], tile_cols, weights["ix"], True, False)
+                mx_product(i_bank[:], h_ops[g], tile_cols, weights["ih"], False, True)
+                i_banks.append(i_bank)
+            sum_banks = []
+            for t in range(PAIR_TILES):
+                j = half * PAIR_TILES + t
+                sum_bank = psum.tile([P, HID], F32, tag="ps")
+                for c in range(CHUNKS):
+                    nc.tensor.matmul(
+                        out=sum_bank[:, c * P : (c + 1) * P],
+                        lhsT=gates[g][:, c, j * P : (j + 1) * P],
+                        rhs=ident_f32[:],
+                        is_transpose=True,
+                        start=(c == 0),
+                        stop=False,
+                    )
+                nc.tensor.matmul(
+                    out=sum_bank[:], lhsT=ident_bf16[:], rhs=m_rows[g][:, j * HID : (j + 1) * HID],
+                    start=False, stop=True,
+                )
+                sum_banks.append(sum_bank)
+            banks[s] = (i_banks, sum_banks)
+
+        def chain(s):
+            i_banks, sum_banks = banks[s]
+            i_arg = arg_pool.tile([P, PAIR_TILES * HID], F32, tag="i_arg")
+            f_arg = arg_pool.tile([P, PAIR_TILES * HID], F32, tag="f_arg")
+            m_t = m_t_pool.tile([P, PAIR_TILES * HID], F32, tag="m_t")
+            tile_cols = [slice(t * HID, (t + 1) * HID) for t in range(PAIR_TILES)]
+            for t, cols in enumerate(tile_cols):
+                nc.vector.tensor_tensor(out=i_arg[:, cols], in0=i_banks[t][:], in1=bi_all[:], op=ALU.add)
+            for t, cols in enumerate(tile_cols):
+                nc.vector.tensor_tensor(out=m_t[:, cols], in0=sum_banks[t][:], in1=i_arg[:, cols], op=ALU.max)
+            for t, cols in enumerate(tile_cols):
+                nc.vector.tensor_tensor(out=f_arg[:, cols], in0=sum_banks[t][:], in1=m_t[:, cols], op=ALU.subtract)
+            nc.gpsimd.tensor_tensor(out=i_arg[:], in0=i_arg[:], in1=m_t[:], op=ALU.subtract)
+            nc.sync.dma_start(out=pair_rows(out_0, s), in_=m_t[:])
+            i_args[s] = i_arg
+            f_args[s] = f_arg
+
+        def exponentials(k):
+            for g in round_groups(k):
+                for s in group_pairs(g):
+                    nc.scalar.activation(out=f_args[s][:], in_=f_args[s][:], func=ACT.Exp)
+                    nc.sync.dma_start(out=pair_rows(out_2, s), in_=f_args[s][:])
+                    nc.scalar.activation(out=i_args[s][:], in_=i_args[s][:], func=ACT.Exp)
+                    nc.sync.dma_start(out=pair_rows(out_1, s), in_=i_args[s][:])
+
         bias_rows = consts.tile([P, P], BF16, tag="bias_rows")
         nc.vector.memset(bias_rows[:], 0.0)
         nc.scalar.dma_start(out=bias_rows[0:CHUNKS, :], in_=b_f.rearrange("(c p) -> c p", p=P))
-
+        warm = consts.tile([P, 1], F32, tag="warm")
+        nc.vector.memset(warm[:], 0.0)
+        nc.scalar.activation(out=warm[:], in_=warm[:], func=ACT.Sigmoid)
         wfx_raw = load_weight(Wf_x)
         wfh_raw = load_weight(Wf_h)
-        x_raw = {}
-        h_raw = {}
-        for g in range(LOAD_AHEAD_GROUPS):
-            x_raw[g] = load_activation(x, g)
-            h_raw[g] = load_activation(h_prev, g)
-        bi_all = consts.tile([P, HID], BF16, tag="bi_all")
-        nc.sync.dma_start(out=bi_all[:], in_=b_i.partition_broadcast(P))
+        load_activations(0)
+        load_activations(1)
 
         bias_bank = psum.tile([P, P], BF16, tag="tr")
         nc.tensor.transpose(bias_bank[:], bias_rows[:], ident_bf16[:])
-        neg_bf = consts.tile([P, CHUNKS], F32, tag="neg_bf")
-        nc.vector.tensor_scalar(
-            out=neg_bf[:], in0=bias_bank[:, 0:CHUNKS], scalar1=-1.0, scalar2=None, op0=ALU.mult
-        )
+        bf_col = consts.tile([P, CHUNKS], F32, tag="bf_col")
+        nc.vector.tensor_copy(out=bf_col[:], in_=bias_bank[:, 0:CHUNKS])
 
-        weights = {}
         weights["fx"] = prepare_weight(wfx_raw, "wfx", nc.scalar.copy)
         weights["fh"] = prepare_weight(wfh_raw, "wfh", nc.scalar.copy)
 
-        x_ops = {}
-        h_ops = {}
-        m_rows = {}
-        e_tiles = {}
-        i_tildes = {}
-        m_ts = {}
-        i_args = {}
-        f_args = {}
-        unclamped = None
+        wix_raw = load_weight(Wi_x)
+        wih_raw = load_weight(Wi_h)
+        bi_all = consts.tile([P, HID], BF16, tag="bi_all")
+        nc.sync.dma_start(out=bi_all[:], in_=b_i.partition_broadcast(P))
+        load_m_prev(0)
 
-        for s in range(-LEAD_TRANSPOSE, N_PAIRS + LAG_EXP):
-            pair_t = s + LEAD_TRANSPOSE
-            pair_q = s + LEAD_QUANTISE
-            pair_l = s + LEAD_LOG
-            pair_e = s - LAG_EXP
-            transposing = pair_t < N_PAIRS
-            quantising = 0 <= pair_q < N_PAIRS
-            coming, k = divmod(pair_l, ROUND_PAIRS)
-            g_f = (coming + 1) * ROUND_GROUPS + k - 2
-            forgetting = k >= 2 and 0 <= g_f < N_GROUPS
-            chain = 0 <= s < N_PAIRS
+        transpose_pair(0)
+        copy_out_pair(0)
+        transpose_pair(1)
+        for q in range(LEAD_PAIRS):
+            copy_out_pair(q + 1)
+            transpose_pair(q + 2)
+            quantise_pair(q)
+            g, half = divmod(q, GROUP_PAIRS)
+            if half == GROUP_PAIRS - 1 and g < ROUND_GROUPS:
+                forget_gate(g)
+            if q + 2 == ROUND_PAIRS - 1:
+                load_activations(2)
+            if q + 2 == LEAD_PAIRS - 1:
+                load_activations(3)
+            if q == ROUND_PAIRS - 1:
+                logarithms(0)
+        weights["ix"] = prepare_weight(wix_raw, "wix", nc.vector.tensor_copy)
+        weights["ih"] = prepare_weight(wih_raw, "wih", nc.vector.tensor_copy)
+        chain_banks(0)
 
-            if pair_t % GROUP_PAIRS == 0:
-                g_load = pair_t // GROUP_PAIRS + LOAD_AHEAD_GROUPS
-                if g_load < N_GROUPS:
-                    x_raw[g_load] = load_activation(x, g_load)
-                    h_raw[g_load] = load_activation(h_prev, g_load)
-            if (s + LEAD_M) % GROUP_PAIRS == 0 and 0 <= s + LEAD_M < N_PAIRS:
-                m_tile = m_pool.tile([P, GROUP_TILES * HID], BF16, tag="m")
-                nc.sync.dma_start(out=m_tile[:], in_=group_rows(m_prev, (s + LEAD_M) // GROUP_PAIRS))
-                m_rows[(s + LEAD_M) // GROUP_PAIRS] = m_tile
-
-            if s == -LEAD_LOG - 3:
-                wix_raw = load_weight(Wi_x)
-                wih_raw = load_weight(Wi_h)
-
-            if k == 0 and 0 <= pair_l < N_PAIRS:
-                for g in range(coming * ROUND_GROUPS, (coming + 1) * ROUND_GROUPS):
-                    flat = e_tiles[g][:].rearrange("p c b -> p (c b)")
-                    nc.scalar.activation(out=flat, in_=flat, func=ACT.Ln, bias=one[:], scale=1.0)
-
-            if chain:
-                g_s, half_s = divmod(s, GROUP_PAIRS)
-                logf_banks = []
-                for t in range(PAIR_TILES):
-                    j = half_s * PAIR_TILES + t
-                    logf_bank = psum.tile([P, HID], F32, tag="lb")
-                    for c in range(CHUNKS):
-                        nc.tensor.transpose(
-                            logf_bank[:, c * P : (c + 1) * P],
-                            e_tiles[g_s][:, c, j * P : (j + 1) * P],
-                            ident_f32[:],
-                        )
-                    logf_banks.append(logf_bank)
-                i_banks = []
-                for t in range(PAIR_TILES):
-                    j = half_s * PAIR_TILES + t
-                    i_bank = psum.tile([P, HID], F32, tag="pi")
-                    tile_cols = slice(j * P, (j + 1) * P)
-                    mx_product(i_bank[:], x_ops[g_s], tile_cols, weights["ix"], True, False)
-                    mx_product(i_bank[:], h_ops[g_s], tile_cols, weights["ih"], False, True)
-                    i_banks.append(i_bank)
-
-            if forgetting:
-                e_tile = e_pool.tile([P, CHUNKS, GROUP_ROWS], F32, tag="e")
-                e_tiles[g_f] = e_tile
-                for c in range(CHUNKS):
-                    f_bank = psum.tile([P, GROUP_ROWS], F32, tag="pf")
-                    chunk_cols = slice(c * P, (c + 1) * P)
-                    mx_product(f_bank[:], weights["fx"], chunk_cols, x_ops[g_f], True, False)
-                    mx_product(f_bank[:], weights["fh"], chunk_cols, h_ops[g_f], False, True)
-                    nc.scalar.activation(
-                        out=e_tiles[g_f][:, c, :], in_=f_bank[:], func=ACT.Exp,
-                        bias=neg_bf[:, c : c + 1], scale=-1.0,
-                    )
-                unclamped = g_f
-
-            if chain:
-                i_tilde = short_pool.tile([P, PAIR_TILES * HID], F32, tag="i_tilde")
-                f_arg = long_pool.tile([P, PAIR_TILES * HID], F32, tag="f_arg")
-                m_t = short_pool.tile([P, PAIR_TILES * HID], F32, tag="m_t")
-                for t in range(PAIR_TILES):
-                    j = half_s * PAIR_TILES + t
-                    cols = slice(t * HID, (t + 1) * HID)
-                    nc.vector.tensor_tensor(out=i_tilde[:, cols], in0=i_banks[t][:], in1=bi_all[:], op=ALU.add)
-                    nc.vector.scalar_tensor_tensor(
-                        out=f_arg[:, cols], in0=logf_banks[t][:], scalar=-1.0,
-                        in1=m_rows[g_s][:, j * HID : (j + 1) * HID], op0=ALU.mult, op1=ALU.add,
-                    )
-            if 0 <= s - 1 < N_PAIRS:
-                i_arg = long_pool.tile([P, PAIR_TILES * HID], F32, tag="i_arg")
-                nc.vector.tensor_tensor(out=i_arg[:], in0=i_tildes[s - 1][:], in1=m_ts[s - 1][:], op=ALU.subtract)
-                i_args[s - 1] = i_arg
-            if quantising:
-                quantise_half(x_ops[pair_q // GROUP_PAIRS], pair_q % GROUP_PAIRS)
-            if quantising:
-                quantise_half(h_ops[pair_q // GROUP_PAIRS], pair_q % GROUP_PAIRS)
-            if unclamped is not None:
-                flat = e_tiles[unclamped][:].rearrange("p c b -> p (c b)")
-                nc.vector.tensor_scalar_min(out=flat, in0=flat, scalar1=E_MAX)
-                unclamped = None
-            if chain:
-                nc.vector.tensor_tensor(out=m_t[:], in0=f_arg[:], in1=i_tilde[:], op=ALU.max)
-                nc.gpsimd.tensor_tensor(out=f_arg[:], in0=f_arg[:], in1=m_t[:], op=ALU.subtract)
-                nc.sync.dma_start(out=pair_rows(out_0, s), in_=m_t[:])
-                i_tildes[s] = i_tilde
-                m_ts[s] = m_t
-                f_args[s] = f_arg
-
-            if 0 <= pair_e < N_PAIRS:
-                nc.scalar.activation(out=i_args[pair_e][:], in_=i_args[pair_e][:], func=ACT.Exp)
-                nc.sync.dma_start(out=pair_rows(out_1, pair_e), in_=i_args[pair_e][:])
-                nc.scalar.activation(out=f_args[pair_e][:], in_=f_args[pair_e][:], func=ACT.Exp)
-                nc.sync.dma_start(out=pair_rows(out_2, pair_e), in_=f_args[pair_e][:])
-
-            if transposing:
-                g_t, half_t = divmod(pair_t, GROUP_PAIRS)
-                if half_t == 0:
-                    x_ops[g_t] = new_operand(x_raw[g_t], codes_pool, "x", "x_grouped")
-                    h_ops[g_t] = new_operand(h_raw[g_t], codes_pool, "h", "h_grouped")
-                x_bank = transpose_half(x_ops[g_t], half_t)
-                h_bank = transpose_half(h_ops[g_t], half_t)
-                copy = nc.vector.tensor_copy if k == 0 else nc.scalar.copy
-                copy_out_half(x_ops[g_t], half_t, x_bank, copy)
-                copy_out_half(h_ops[g_t], half_t, h_bank, copy)
-
-            if s == -LEAD_LOG:
-                weights["ix"] = prepare_weight(wix_raw, "wix", nc.vector.tensor_copy)
-                weights["ih"] = prepare_weight(wih_raw, "wih", nc.vector.tensor_copy)
+        for k in range(N_ROUNDS):
+            load_m_prev(k + 1)
+            for g in round_groups(k + 1):
+                forget_gate(g)
+            logarithms(k + 1)
+            for s in range(k * ROUND_PAIRS, (k + 1) * ROUND_PAIRS):
+                q = s + LEAD_PAIRS
+                quantise_pair(q)
+                chain(s)
+                copy_out_pair(q + 1)
+                if s + 1 < N_PAIRS:
+                    chain_banks(s + 1)
+                transpose_pair(q + 2)
+            load_activations(k + 4)
+            exponentials(k)

@@ -28,7 +28,7 @@ ROUND_PAIRS = ROUND_GROUPS * GROUP_PAIRS
 N_GROUPS = BATCH // GROUP_ROWS
 N_ROUNDS = N_GROUPS // ROUND_GROUPS
 N_PAIRS = BATCH // PAIR_ROWS
-LEAD_PAIRS = 2 * ROUND_PAIRS
+assert ROUND_GROUPS == 2
 
 SIGMOID_MIN = 1.0e-8
 
@@ -43,11 +43,11 @@ def tile_slstmlayer_pa_t_kernel(
         consts = ctx.enter_context(tc.tile_pool(name="consts", bufs=1))
         raws = ctx.enter_context(tc.tile_pool(name="raws", bufs=4 * ROUND_GROUPS))
         m_pool = ctx.enter_context(tc.tile_pool(name="m_pool", bufs=2 * ROUND_GROUPS))
-        grouped_pool = ctx.enter_context(tc.tile_pool(name="grouped_pool", bufs=3))
+        grouped_pool = ctx.enter_context(tc.tile_pool(name="grouped_pool", bufs=2))
         codes_pool = ctx.enter_context(tc.tile_pool(name="codes_pool", bufs=3 * ROUND_GROUPS))
         gate_pool = ctx.enter_context(tc.tile_pool(name="gate_pool", bufs=2 * ROUND_GROUPS))
         arg_pool = ctx.enter_context(tc.tile_pool(name="arg_pool", bufs=ROUND_PAIRS + 3))
-        m_t_pool = ctx.enter_context(tc.tile_pool(name="m_t_pool", bufs=3))
+        m_t_pool = ctx.enter_context(tc.tile_pool(name="m_t_pool", bufs=4))
         psum = ctx.enter_context(tc.psum_pool(name="psum", bufs=2))
         ctx.enter_context(tc.manual_schedule())
 
@@ -85,22 +85,26 @@ def tile_slstmlayer_pa_t_kernel(
         def group_pairs(g):
             return range(g * GROUP_PAIRS, (g + 1) * GROUP_PAIRS)
 
+        def load_group_activations(g):
+            x_raw[g] = raws.tile([P, GROUP_TILES * FEAT], BF16, tag="raw", name="x_raw")
+            load_group(x_raw[g], x, g)
+            h_raw[g] = raws.tile([P, GROUP_TILES * FEAT], BF16, tag="raw", name="h_raw")
+            load_group(h_raw[g], h_prev, g)
+
         def load_activations(k):
             for g in round_groups(k):
-                x_raw[g] = raws.tile([P, GROUP_TILES * FEAT], BF16, tag="raw", name="x_raw")
-                load_group(x_raw[g], x, g)
-                h_raw[g] = raws.tile([P, GROUP_TILES * FEAT], BF16, tag="raw", name="h_raw")
-                load_group(h_raw[g], h_prev, g)
+                load_group_activations(g)
 
         def load_m_prev(k):
             for g in round_groups(k):
                 m_rows[g] = m_pool.tile([P, GROUP_TILES * HID], BF16, tag="m", name="m_rows")
                 load_group(m_rows[g], m_prev, g)
 
-        def new_operand(raw, pool, name, grouped_tag):
+        def new_operand(raw, pool, name, side):
+            grouped = grouped_pool.tile([P, 4 * GROUP_ROWS], BF16, tag=side + "_grouped", align_bytes=64)
             codes = pool.tile([P, GROUP_ROWS], U32, tag=name + "_codes", align_bytes=64)
             scales = pool.tile([P, GROUP_ROWS], U8, tag=name + "_scales", align_bytes=64)
-            return {"raw": raw, "codes": codes, "scales": scales, "grouped_tag": grouped_tag, "grouped": {}}
+            return {"raw": raw, "grouped": grouped, "codes": codes, "scales": scales}
 
         def transpose_half(operand, half, bank_tag):
             words = operand["raw"][:].bitcast(F32)
@@ -114,27 +118,19 @@ def tile_slstmlayer_pa_t_kernel(
             return bank
 
         def copy_out_half(operand, half, bank, copy):
-            grouped = grouped_pool.tile([P, 4 * PAIR_ROWS], BF16, tag=operand["grouped_tag"], align_bytes=64)
-            copy(
-                out=grouped[:].bitcast(F32).rearrange("p (r u) -> p r u", u=2),
-                in_=bank[:].rearrange("p u r -> p r u"),
-            )
-            operand["grouped"][half] = grouped
+            words = operand["grouped"][:].bitcast(F32)[:, half * 2 * PAIR_ROWS : (half + 1) * 2 * PAIR_ROWS]
+            copy(out=words.rearrange("p (r u) -> p r u", u=2), in_=bank[:].rearrange("p u r -> p r u"))
 
-        def quantise_half(operand, half):
-            rows = slice(half * PAIR_ROWS, (half + 1) * PAIR_ROWS)
+        def quantise(operand):
             nc.vector.quantize_mx(
-                out=operand["codes"][:, rows].bitcast(FP8X4),
-                scales=operand["scales"][:, rows],
-                in_=operand["grouped"][half][:],
+                out=operand["codes"][:].bitcast(FP8X4), scales=operand["scales"][:], in_=operand["grouped"][:]
             )
 
-        def prepare_weight(raw, name, second_copy):
-            operand = new_operand(raw, consts, name, "w_grouped")
+        def prepare_weight(raw, name, side, second_copy):
+            operand = new_operand(raw, consts, name, side)
             copy_out_half(operand, 0, transpose_half(operand, 0, "pi"), nc.vector.tensor_copy)
             copy_out_half(operand, 1, transpose_half(operand, 1, "pi"), second_copy)
-            quantise_half(operand, 0)
-            quantise_half(operand, 1)
+            quantise(operand)
             return operand
 
         def mx_product(out, stationary, stationary_cols, moving, start, stop):
@@ -152,7 +148,6 @@ def tile_slstmlayer_pa_t_kernel(
         x_ops = {}
         h_ops = {}
         gates = {}
-        word_banks = {}
         banks = {}
         i_args = {}
         f_args = {}
@@ -178,26 +173,16 @@ def tile_slstmlayer_pa_t_kernel(
                 flat = gates[g][:].rearrange("p c b -> p (c b)")
                 nc.scalar.activation(out=flat, in_=flat, func=ACT.Ln)
 
-        def transpose_pair(q):
-            if q < N_PAIRS:
-                g, half = divmod(q, GROUP_PAIRS)
-                if half == 0:
-                    x_ops[g] = new_operand(x_raw[g], codes_pool, "x", "x_grouped")
-                    h_ops[g] = new_operand(h_raw[g], codes_pool, "h", "h_grouped")
-                word_banks[q] = (transpose_half(x_ops[g], half, "tr"), transpose_half(h_ops[g], half, "tr"))
-
-        def copy_out_pair(q):
-            if q < N_PAIRS:
-                g, half = divmod(q, GROUP_PAIRS)
-                x_bank, h_bank = word_banks[q]
+        def prepare_group(g, h_copy):
+            x_ops[g] = new_operand(x_raw[g], codes_pool, "x", "x")
+            h_ops[g] = new_operand(h_raw[g], codes_pool, "h", "h")
+            for half in range(GROUP_PAIRS):
+                x_bank = transpose_half(x_ops[g], half, "tr")
+                h_bank = transpose_half(h_ops[g], half, "tr")
                 copy_out_half(x_ops[g], half, x_bank, nc.vector.tensor_copy)
-                copy_out_half(h_ops[g], half, h_bank, nc.vector.tensor_copy)
-
-        def quantise_pair(q):
-            if q < N_PAIRS:
-                g, half = divmod(q, GROUP_PAIRS)
-                quantise_half(x_ops[g], half)
-                quantise_half(h_ops[g], half)
+                copy_out_half(h_ops[g], half, h_bank, h_copy)
+            quantise(x_ops[g])
+            quantise(h_ops[g])
 
         def chain_banks(s):
             g, half = divmod(s, GROUP_PAIRS)
@@ -262,41 +247,35 @@ def tile_slstmlayer_pa_t_kernel(
         nc.scalar.activation(out=warm[:], in_=warm[:], func=ACT.Sigmoid)
         wfx_raw = load_weight(Wf_x)
         wfh_raw = load_weight(Wf_h)
-        load_activations(0)
-        load_activations(1)
+        load_group_activations(0)
 
         bias_bank = psum.tile([P, P], BF16, tag="tr")
         nc.tensor.transpose(bias_bank[:], bias_rows[:], ident_bf16[:])
         bf_col = consts.tile([P, CHUNKS], F32, tag="bf_col")
         nc.vector.tensor_copy(out=bf_col[:], in_=bias_bank[:, 0:CHUNKS])
 
-        weights["fx"] = prepare_weight(wfx_raw, "wfx", nc.scalar.copy)
-        weights["fh"] = prepare_weight(wfh_raw, "wfh", nc.scalar.copy)
+        weights["fx"] = prepare_weight(wfx_raw, "wfx", "x", nc.scalar.copy)
+        weights["fh"] = prepare_weight(wfh_raw, "wfh", "h", nc.scalar.copy)
 
         wix_raw = load_weight(Wi_x)
+        load_group_activations(1)
         wih_raw = load_weight(Wi_h)
         bi_all = consts.tile([P, HID], BF16, tag="bi_all")
         nc.sync.dma_start(out=bi_all[:], in_=b_i.partition_broadcast(P))
+        load_activations(1)
         load_m_prev(0)
 
-        transpose_pair(0)
-        copy_out_pair(0)
-        transpose_pair(1)
-        for q in range(LEAD_PAIRS):
-            copy_out_pair(q + 1)
-            transpose_pair(q + 2)
-            quantise_pair(q)
-            g, half = divmod(q, GROUP_PAIRS)
-            if half == GROUP_PAIRS - 1 and g < ROUND_GROUPS:
-                forget_gate(g)
-            if q + 2 == ROUND_PAIRS - 1:
-                load_activations(2)
-            if q + 2 == LEAD_PAIRS - 1:
-                load_activations(3)
-            if q == ROUND_PAIRS - 1:
-                logarithms(0)
-        weights["ix"] = prepare_weight(wix_raw, "wix", nc.vector.tensor_copy)
-        weights["ih"] = prepare_weight(wih_raw, "wih", nc.vector.tensor_copy)
+        prepare_group(0, nc.scalar.copy)
+        weights["ix"] = prepare_weight(wix_raw, "wix", "x", nc.vector.tensor_copy)
+        forget_gate(0)
+        prepare_group(1, nc.vector.tensor_copy)
+        weights["ih"] = prepare_weight(wih_raw, "wih", "h", nc.vector.tensor_copy)
+        forget_gate(1)
+        logarithms(0)
+        load_activations(2)
+        for g in round_groups(1):
+            prepare_group(g, nc.vector.tensor_copy)
+        load_activations(3)
         chain_banks(0)
 
         for k in range(N_ROUNDS):
@@ -305,12 +284,9 @@ def tile_slstmlayer_pa_t_kernel(
                 forget_gate(g)
             logarithms(k + 1)
             for s in range(k * ROUND_PAIRS, (k + 1) * ROUND_PAIRS):
-                q = s + LEAD_PAIRS
-                quantise_pair(q)
                 chain(s)
-                copy_out_pair(q + 1)
                 if s + 1 < N_PAIRS:
                     chain_banks(s + 1)
-                transpose_pair(q + 2)
-            load_activations(k + 4)
+            for g in round_groups(k + 2):
+                prepare_group(g, nc.vector.tensor_copy)
             exponentials(k)

@@ -148,6 +148,7 @@ def tile_slstmlayer_pa_t_kernel(
         x_ops = {}
         h_ops = {}
         gates = {}
+        word_banks = {}
         banks = {}
         i_args = {}
         f_args = {}
@@ -173,16 +174,28 @@ def tile_slstmlayer_pa_t_kernel(
                 flat = gates[g][:].rearrange("p c b -> p (c b)")
                 nc.scalar.activation(out=flat, in_=flat, func=ACT.Ln)
 
-        def prepare_group(g, h_copy):
+        def start_group(g, bank_tag):
             x_ops[g] = new_operand(x_raw[g], codes_pool, "x", "x")
             h_ops[g] = new_operand(h_raw[g], codes_pool, "h", "h")
-            for half in range(GROUP_PAIRS):
-                x_bank = transpose_half(x_ops[g], half, "tr")
-                h_bank = transpose_half(h_ops[g], half, "tr")
-                copy_out_half(x_ops[g], half, x_bank, nc.vector.tensor_copy)
-                copy_out_half(h_ops[g], half, h_bank, h_copy)
+            word_banks[g] = (transpose_half(x_ops[g], 0, bank_tag), transpose_half(h_ops[g], 0, bank_tag))
+
+        def middle_group(g, h_copy):
+            x_bank, h_bank = word_banks[g]
+            copy_out_half(x_ops[g], 0, x_bank, nc.vector.tensor_copy)
+            copy_out_half(h_ops[g], 0, h_bank, h_copy)
+            word_banks[g] = (transpose_half(x_ops[g], 1, "tr"), transpose_half(h_ops[g], 1, "tr"))
+
+        def finish_group(g, h_copy):
+            x_bank, h_bank = word_banks[g]
+            copy_out_half(x_ops[g], 1, x_bank, nc.vector.tensor_copy)
+            copy_out_half(h_ops[g], 1, h_bank, h_copy)
             quantise(x_ops[g])
             quantise(h_ops[g])
+
+        def prepare_group(g, h_copy):
+            start_group(g, "tr")
+            middle_group(g, h_copy)
+            finish_group(g, h_copy)
 
         def chain_banks(s):
             g, half = divmod(s, GROUP_PAIRS)
@@ -231,13 +244,11 @@ def tile_slstmlayer_pa_t_kernel(
             i_args[s] = i_arg
             f_args[s] = f_arg
 
-        def exponentials(k):
-            for g in round_groups(k):
-                for s in group_pairs(g):
-                    nc.scalar.activation(out=f_args[s][:], in_=f_args[s][:], func=ACT.Exp)
-                    nc.sync.dma_start(out=pair_rows(out_2, s), in_=f_args[s][:])
-                    nc.scalar.activation(out=i_args[s][:], in_=i_args[s][:], func=ACT.Exp)
-                    nc.sync.dma_start(out=pair_rows(out_1, s), in_=i_args[s][:])
+        def exponentials(s):
+            nc.scalar.activation(out=f_args[s][:], in_=f_args[s][:], func=ACT.Exp)
+            nc.sync.dma_start(out=pair_rows(out_2, s), in_=f_args[s][:])
+            nc.scalar.activation(out=i_args[s][:], in_=i_args[s][:], func=ACT.Exp)
+            nc.sync.dma_start(out=pair_rows(out_1, s), in_=i_args[s][:])
 
         bias_rows = consts.tile([P, P], BF16, tag="bias_rows")
         nc.vector.memset(bias_rows[:], 0.0)
@@ -266,15 +277,19 @@ def tile_slstmlayer_pa_t_kernel(
         load_m_prev(0)
 
         prepare_group(0, nc.scalar.copy)
+        start_group(1, "ps")
         weights["ix"] = prepare_weight(wix_raw, "wix", "x", nc.vector.tensor_copy)
         forget_gate(0)
-        prepare_group(1, nc.vector.tensor_copy)
+        middle_group(1, nc.vector.tensor_copy)
+        finish_group(1, nc.vector.tensor_copy)
+        start_group(2, "ps")
         weights["ih"] = prepare_weight(wih_raw, "wih", "h", nc.vector.tensor_copy)
         forget_gate(1)
         logarithms(0)
         load_activations(2)
-        for g in round_groups(1):
-            prepare_group(g, nc.vector.tensor_copy)
+        middle_group(2, nc.vector.tensor_copy)
+        finish_group(2, nc.vector.tensor_copy)
+        prepare_group(3, nc.vector.tensor_copy)
         load_activations(3)
         chain_banks(0)
 
@@ -283,10 +298,21 @@ def tile_slstmlayer_pa_t_kernel(
             for g in round_groups(k + 1):
                 forget_gate(g)
             logarithms(k + 1)
-            for s in range(k * ROUND_PAIRS, (k + 1) * ROUND_PAIRS):
+            round_pairs = range(k * ROUND_PAIRS, (k + 1) * ROUND_PAIRS)
+            last_round = k == N_ROUNDS - 1
+            for s in round_pairs:
                 chain(s)
+                if s == round_pairs[-1] and k + 2 < N_ROUNDS:
+                    start_group((k + 2) * ROUND_GROUPS, "tr")
                 if s + 1 < N_PAIRS:
                     chain_banks(s + 1)
+                if last_round:
+                    exponentials(s)
             for g in round_groups(k + 2):
-                prepare_group(g, nc.vector.tensor_copy)
-            exponentials(k)
+                if g > (k + 2) * ROUND_GROUPS:
+                    start_group(g, "tr")
+                middle_group(g, nc.vector.tensor_copy)
+                finish_group(g, nc.vector.tensor_copy)
+            if not last_round:
+                for s in round_pairs:
+                    exponentials(s)

@@ -30,7 +30,7 @@ N_ROUNDS = N_GROUPS // ROUND_GROUPS
 N_PAIRS = BATCH // PAIR_ROWS
 assert ROUND_GROUPS == 2
 
-SIGMOID_MIN = 1.0e-8
+E_MAX = 1.0e8 - 1.0
 
 FLOPS = 2 * BATCH * HID * FEAT * 4
 
@@ -81,9 +81,6 @@ def tile_slstmlayer_pa_t_kernel(
 
         def round_groups(k):
             return range(k * ROUND_GROUPS, (k + 1) * ROUND_GROUPS) if k < N_ROUNDS else ()
-
-        def group_pairs(g):
-            return range(g * GROUP_PAIRS, (g + 1) * GROUP_PAIRS)
 
         def load_group_activations(g):
             x_raw[g] = raws.tile([P, GROUP_TILES * FEAT], BF16, tag="raw", name="x_raw")
@@ -150,8 +147,7 @@ def tile_slstmlayer_pa_t_kernel(
         gates = {}
         word_banks = {}
         banks = {}
-        i_args = {}
-        f_args = {}
+        pair_args = {}
 
         def forget_gate(g):
             gates[g] = gate_pool.tile([P, CHUNKS, GROUP_ROWS], F32, tag="gate", name="gate")
@@ -161,18 +157,18 @@ def tile_slstmlayer_pa_t_kernel(
                 mx_product(f_bank[:], weights["fx"], chunk_cols, x_ops[g], True, False)
                 mx_product(f_bank[:], weights["fh"], chunk_cols, h_ops[g], False, True)
                 nc.scalar.activation(
-                    out=gates[g][:, c, :], in_=f_bank[:], func=ACT.Sigmoid,
-                    bias=bf_col[:, c : c + 1], scale=1.0,
+                    out=gates[g][:, c, :], in_=f_bank[:], func=ACT.Exp,
+                    bias=neg_bf[:, c : c + 1], scale=-1.0,
                 )
                 nc.gpsimd.tensor_scalar(
                     out=gates[g][:, c, :], in0=gates[g][:, c, :],
-                    scalar1=1.0, scalar2=SIGMOID_MIN, op0=ALU.min, op1=ALU.max,
+                    scalar1=E_MAX, scalar2=0.0, op0=ALU.min, op1=ALU.max,
                 )
 
         def logarithms(k):
             for g in round_groups(k):
                 flat = gates[g][:].rearrange("p c b -> p (c b)")
-                nc.scalar.activation(out=flat, in_=flat, func=ACT.Ln)
+                nc.scalar.activation(out=flat, in_=flat, func=ACT.Ln, bias=one[:], scale=1.0)
 
         def start_group(g, bank_tag):
             x_ops[g] = new_operand(x_raw[g], codes_pool, "x", "x")
@@ -221,7 +217,7 @@ def tile_slstmlayer_pa_t_kernel(
                         stop=False,
                     )
                 nc.tensor.matmul(
-                    out=sum_bank[:], lhsT=ident_bf16[:], rhs=m_rows[g][:, j * HID : (j + 1) * HID],
+                    out=sum_bank[:], lhsT=neg_ident[:], rhs=m_rows[g][:, j * HID : (j + 1) * HID],
                     start=False, stop=True,
                 )
                 sum_banks.append(sum_bank)
@@ -229,41 +225,50 @@ def tile_slstmlayer_pa_t_kernel(
 
         def chain(s):
             i_banks, sum_banks = banks[s]
-            i_arg = arg_pool.tile([P, PAIR_TILES * HID], F32, tag="i_arg")
-            f_arg = arg_pool.tile([P, PAIR_TILES * HID], F32, tag="f_arg")
+            args = arg_pool.tile([P, 2, PAIR_TILES * HID], F32, tag="args")
+            i_arg = args[:, 0, :]
+            f_arg = args[:, 1, :]
             m_t = m_t_pool.tile([P, PAIR_TILES * HID], F32, tag="m_t")
             tile_cols = [slice(t * HID, (t + 1) * HID) for t in range(PAIR_TILES)]
             for t, cols in enumerate(tile_cols):
                 nc.vector.tensor_tensor(out=i_arg[:, cols], in0=i_banks[t][:], in1=bi_all[:], op=ALU.add)
             for t, cols in enumerate(tile_cols):
-                nc.vector.tensor_tensor(out=m_t[:, cols], in0=sum_banks[t][:], in1=i_arg[:, cols], op=ALU.max)
+                nc.vector.scalar_tensor_tensor(
+                    out=m_t[:, cols], in0=sum_banks[t][:], scalar=-1.0, in1=i_arg[:, cols], op0=ALU.mult, op1=ALU.max
+                )
             for t, cols in enumerate(tile_cols):
-                nc.vector.tensor_tensor(out=f_arg[:, cols], in0=sum_banks[t][:], in1=m_t[:, cols], op=ALU.subtract)
-            nc.gpsimd.tensor_tensor(out=i_arg[:], in0=i_arg[:], in1=m_t[:], op=ALU.subtract)
+                nc.vector.scalar_tensor_tensor(
+                    out=f_arg[:, cols], in0=sum_banks[t][:], scalar=-1.0, in1=m_t[:, cols], op0=ALU.mult, op1=ALU.subtract
+                )
+            nc.gpsimd.tensor_tensor(out=i_arg, in0=i_arg, in1=m_t[:], op=ALU.subtract)
             nc.sync.dma_start(out=pair_rows(out_0, s), in_=m_t[:])
-            i_args[s] = i_arg
-            f_args[s] = f_arg
+            pair_args[s] = args
 
         def exponentials(s):
-            nc.scalar.activation(out=f_args[s][:], in_=f_args[s][:], func=ACT.Exp)
-            nc.sync.dma_start(out=pair_rows(out_2, s), in_=f_args[s][:])
-            nc.scalar.activation(out=i_args[s][:], in_=i_args[s][:], func=ACT.Exp)
-            nc.sync.dma_start(out=pair_rows(out_1, s), in_=i_args[s][:])
+            both = pair_args[s][:].rearrange("p a w -> p (a w)")
+            nc.scalar.activation(out=both, in_=both, func=ACT.Exp)
+            nc.sync.dma_start(out=pair_rows(out_1, s), in_=pair_args[s][:, 0, :])
+            nc.sync.dma_start(out=pair_rows(out_2, s), in_=pair_args[s][:, 1, :])
 
         bias_rows = consts.tile([P, P], BF16, tag="bias_rows")
         nc.vector.memset(bias_rows[:], 0.0)
         nc.scalar.dma_start(out=bias_rows[0:CHUNKS, :], in_=b_f.rearrange("(c p) -> c p", p=P))
+        one = consts.tile([P, 1], F32, tag="one")
+        nc.vector.memset(one[:], 1.0)
         warm = consts.tile([P, 1], F32, tag="warm")
-        nc.vector.memset(warm[:], 0.0)
-        nc.scalar.activation(out=warm[:], in_=warm[:], func=ACT.Sigmoid)
+        nc.scalar.activation(out=warm[:], in_=one[:], func=ACT.Exp)
+        neg_ident = consts.tile([P, P], BF16, tag="neg_ident")
+        nc.vector.tensor_scalar(out=neg_ident[:], in0=ident_bf16[:], scalar1=-1.0, scalar2=None, op0=ALU.mult)
         wfx_raw = load_weight(Wf_x)
         wfh_raw = load_weight(Wf_h)
         load_group_activations(0)
 
         bias_bank = psum.tile([P, P], BF16, tag="tr")
         nc.tensor.transpose(bias_bank[:], bias_rows[:], ident_bf16[:])
-        bf_col = consts.tile([P, CHUNKS], F32, tag="bf_col")
-        nc.vector.tensor_copy(out=bf_col[:], in_=bias_bank[:, 0:CHUNKS])
+        neg_bf = consts.tile([P, CHUNKS], F32, tag="neg_bf")
+        nc.vector.tensor_scalar(
+            out=neg_bf[:], in0=bias_bank[:, 0:CHUNKS], scalar1=-1.0, scalar2=None, op0=ALU.mult
+        )
 
         weights["fx"] = prepare_weight(wfx_raw, "wfx", "x", nc.scalar.copy)
         weights["fh"] = prepare_weight(wfh_raw, "wfh", "h", nc.scalar.copy)
@@ -299,17 +304,18 @@ def tile_slstmlayer_pa_t_kernel(
                 forget_gate(g)
             logarithms(k + 1)
             round_pairs = range(k * ROUND_PAIRS, (k + 1) * ROUND_PAIRS)
+            coming = round_groups(k + 2)
             last_round = k == N_ROUNDS - 1
             for s in round_pairs:
                 chain(s)
-                if s == round_pairs[-1] and k + 2 < N_ROUNDS:
-                    start_group((k + 2) * ROUND_GROUPS, "tr")
+                if s == round_pairs[-1] and coming:
+                    start_group(coming[0], "tr")
                 if s + 1 < N_PAIRS:
                     chain_banks(s + 1)
                 if last_round:
                     exponentials(s)
-            for g in round_groups(k + 2):
-                if g > (k + 2) * ROUND_GROUPS:
+            for g in coming:
+                if g != coming[0]:
                     start_group(g, "tr")
                 middle_group(g, nc.vector.tensor_copy)
                 finish_group(g, nc.vector.tensor_copy)

from contextlib import ExitStack

import concourse.mybir as mybir
from concourse.masks import make_identity

F32 = mybir.dt.float32
BF16 = mybir.dt.bfloat16
U32 = mybir.dt.uint32
U8 = mybir.dt.uint8
FP8X4 = mybir.dt.float8_e4m3fn_x4
ACT = mybir.ActivationFunctionType
ALU = mybir.AluOpType

P = 128
BATCH = 4096
FEAT = 512
HID = 512
WORDS = FEAT // 2
CHUNKS = HID // P

PAIR_TILES = 2
PAIR_ROWS = PAIR_TILES * P
GROUP_PAIRS = 2
GROUP_TILES = GROUP_PAIRS * PAIR_TILES
GROUP_ROWS = GROUP_TILES * P
ROUND_GROUPS = 2
ROUND_PAIRS = ROUND_GROUPS * GROUP_PAIRS
N_GROUPS = BATCH // GROUP_ROWS
N_ROUNDS = N_GROUPS // ROUND_GROUPS
N_PAIRS = BATCH // PAIR_ROWS
assert ROUND_GROUPS == 2

E_MAX = 1.0e8 - 1.0

FLOPS = 2 * BATCH * HID * FEAT * 4


def tile_slstmlayer_pa_t_kernel(
    tc, x, h_prev, m_prev, Wi_x, b_i, Wi_h, Wf_x, b_f, Wf_h, out_0, out_1, out_2
):
    nc = tc.nc
    with ExitStack() as ctx:
        consts = ctx.enter_context(tc.tile_pool(name="consts", bufs=1))
        raws = ctx.enter_context(tc.tile_pool(name="raws", bufs=4 * ROUND_GROUPS))
        m_pool = ctx.enter_context(tc.tile_pool(name="m_pool", bufs=2 * ROUND_GROUPS))
        grouped_pool = ctx.enter_context(tc.tile_pool(name="grouped_pool", bufs=2))
        codes_pool = ctx.enter_context(tc.tile_pool(name="codes_pool", bufs=3 * ROUND_GROUPS))
        gate_pool = ctx.enter_context(tc.tile_pool(name="gate_pool", bufs=2 * ROUND_GROUPS))
        arg_pool = ctx.enter_context(tc.tile_pool(name="arg_pool", bufs=ROUND_PAIRS + 3))
        m_t_pool = ctx.enter_context(tc.tile_pool(name="m_t_pool", bufs=4))
        psum = ctx.enter_context(tc.psum_pool(name="psum", bufs=2))
        ctx.enter_context(tc.manual_schedule())

        ident_f32 = consts.tile([P, P], F32, tag="ident_f32")
        make_identity(nc, ident_f32[:])
        ident_bf16 = consts.tile([P, P], BF16, tag="ident_bf16")
        make_identity(nc, ident_bf16[:])

        def pair_rows(dram, s):
            rows = dram[s * PAIR_ROWS : (s + 1) * PAIR_ROWS, :]
            return rows.rearrange("(p t) k -> p (t k)", t=PAIR_TILES)

        def load_group(rows_tile, dram, g):
            rows = dram[g * GROUP_ROWS : (g + 1) * GROUP_ROWS, :]
            nc.sync.dma_start(
                out=rows_tile[:].rearrange("p (a w) -> p a w", a=GROUP_PAIRS),
                in_=rows.rearrange("(a p t) k -> p a (t k)", a=GROUP_PAIRS, t=PAIR_TILES),
            )

        def load_weight(w):
            raw = raws.tile([P, GROUP_TILES * FEAT], BF16, tag="w_raw", bufs=2)
            nc.sync.dma_start(
                out=raw[:].rearrange("p (c k) -> p c k", c=CHUNKS),
                in_=w.rearrange("(c p) k -> p c k", p=P),
            )
            return raw

        x_raw = {}
        h_raw = {}
        m_rows = {}

        def round_groups(k):
            return range(k * ROUND_GROUPS, (k + 1) * ROUND_GROUPS) if k < N_ROUNDS else ()

        def load_group_activations(g):
            x_raw[g] = raws.tile([P, GROUP_TILES * FEAT], BF16, tag="raw", name="x_raw")
            load_group(x_raw[g], x, g)
            h_raw[g] = raws.tile([P, GROUP_TILES * FEAT], BF16, tag="raw", name="h_raw")
            load_group(h_raw[g], h_prev, g)

        def load_activations(k):
            for g in round_groups(k):
                load_group_activations(g)

        def load_m_prev(k):
            for g in round_groups(k):
                m_rows[g] = m_pool.tile([P, GROUP_TILES * HID], BF16, tag="m", name="m_rows")
                load_group(m_rows[g], m_prev, g)

        def new_operand(raw, pool, name, side):
            grouped = grouped_pool.tile([P, 4 * GROUP_ROWS], BF16, tag=side + "_grouped", align_bytes=64)
            codes = pool.tile([P, GROUP_ROWS], U32, tag=name + "_codes", align_bytes=64)
            scales = pool.tile([P, GROUP_ROWS], U8, tag=name + "_scales", align_bytes=64)
            return {"raw": raw, "grouped": grouped, "codes": codes, "scales": scales}

        def transpose_half(operand, half, bank_tag):
            words = operand["raw"][:].bitcast(F32)
            bank = psum.tile([P, 2, PAIR_ROWS], F32, tag=bank_tag)
            for t in range(PAIR_TILES):
                for u in range(2):
                    first = (half * PAIR_TILES + t) * WORDS + u * P
                    nc.tensor.transpose(
                        bank[:, u, t * P : (t + 1) * P], words[:, first : first + P], ident_f32[:]
                    )
            return bank

        def copy_out_half(operand, half, bank, copy):
            words = operand["grouped"][:].bitcast(F32)[:, half * 2 * PAIR_ROWS : (half + 1) * 2 * PAIR_ROWS]
            copy(out=words.rearrange("p (r u) -> p r u", u=2), in_=bank[:].rearrange("p u r -> p r u"))

        def quantise(operand):
            nc.vector.quantize_mx(
                out=operand["codes"][:].bitcast(FP8X4), scales=operand["scales"][:], in_=operand["grouped"][:]
            )

        def prepare_weight(raw, name, side, second_copy):
            operand = new_operand(raw, consts, name, side)
            copy_out_half(operand, 0, transpose_half(operand, 0, "pi"), nc.vector.tensor_copy)
            copy_out_half(operand, 1, transpose_half(operand, 1, "pi"), second_copy)
            quantise(operand)
            return operand

        def mx_product(out, stationary, stationary_cols, moving, start, stop):
            nc.tensor.matmul_mx(
                out=out,
                lhsT=stationary["codes"][:, stationary_cols].bitcast(FP8X4),
                lhsT_scale=stationary["scales"][:, stationary_cols],
                rhs=moving["codes"][:].bitcast(FP8X4),
                rhs_scale=moving["scales"][:],
                start=start,
                stop=stop,
            )

        weights = {}
        x_ops = {}
        h_ops = {}
        gates = {}
        word_banks = {}
        banks = {}
        pair_args = {}

        def forget_gate(g):
            gates[g] = gate_pool.tile([P, CHUNKS, GROUP_ROWS], F32, tag="gate", name="gate")
            for c in range(CHUNKS):
                f_bank = psum.tile([P, GROUP_ROWS], F32, tag="pf")
                chunk_cols = slice(c * P, (c + 1) * P)
                mx_product(f_bank[:], weights["fx"], chunk_cols, x_ops[g], True, False)
                mx_product(f_bank[:], weights["fh"], chunk_cols, h_ops[g], False, True)
                nc.scalar.activation(
                    out=gates[g][:, c, :], in_=f_bank[:], func=ACT.Exp,
                    bias=neg_bf[:, c : c + 1], scale=-1.0,
                )
                nc.gpsimd.tensor_scalar(
                    out=gates[g][:, c, :], in0=gates[g][:, c, :],
                    scalar1=E_MAX, scalar2=0.0, op0=ALU.min, op1=ALU.max,
                )

        def logarithms(k):
            for g in round_groups(k):
                flat = gates[g][:].rearrange("p c b -> p (c b)")
                nc.scalar.activation(out=flat, in_=flat, func=ACT.Ln, bias=one[:], scale=1.0)

        def start_group(g, bank_tag):
            x_ops[g] = new_operand(x_raw[g], codes_pool, "x", "x")
            h_ops[g] = new_operand(h_raw[g], codes_pool, "h", "h")
            word_banks[g] = (transpose_half(x_ops[g], 0, bank_tag), transpose_half(h_ops[g], 0, bank_tag))

        def middle_group(g, h_copy):
            x_bank, h_bank = word_banks[g]
            copy_out_half(x_ops[g], 0, x_bank, nc.vector.tensor_copy)
            copy_out_half(h_ops[g], 0, h_bank, h_copy)
            word_banks[g] = (transpose_half(x_ops[g], 1, "tr"), transpose_half(h_ops[g], 1, "tr"))

        def finish_group(g, h_copy):
            x_bank, h_bank = word_banks[g]
            copy_out_half(x_ops[g], 1, x_bank, nc.vector.tensor_copy)
            copy_out_half(h_ops[g], 1, h_bank, h_copy)
            quantise(x_ops[g])
            quantise(h_ops[g])

        def prepare_group(g, h_copy):
            start_group(g, "tr")
            middle_group(g, h_copy)
            finish_group(g, h_copy)

        def chain_banks(s):
            g, half = divmod(s, GROUP_PAIRS)
            i_banks = []
            for t in range(PAIR_TILES):
                j = half * PAIR_TILES + t
                i_bank = psum.tile([P, HID], F32, tag="pi")
                tile_cols = slice(j * P, (j + 1) * P)
                mx_product(i_bank[:], x_ops[g], tile_cols, weights["ix"], True, False)
                mx_product(i_bank[:], h_ops[g], tile_cols, weights["ih"], False, True)
                i_banks.append(i_bank)
            sum_banks = []
            for t in range(PAIR_TILES):
                j = half * PAIR_TILES + t
                sum_bank = psum.tile([P, HID], F32, tag="ps")
                for c in range(CHUNKS):
                    nc.tensor.matmul(
                        out=sum_bank[:, c * P : (c + 1) * P],
                        lhsT=gates[g][:, c, j * P : (j + 1) * P],
                        rhs=ident_f32[:],
                        is_transpose=True,
                        start=(c == 0),
                        stop=False,
                    )
                nc.tensor.matmul(
                    out=sum_bank[:], lhsT=neg_ident[:], rhs=m_rows[g][:, j * HID : (j + 1) * HID],
                    start=False, stop=True,
                )
                sum_banks.append(sum_bank)
            banks[s] = (i_banks, sum_banks)

        def chain(s):
            i_banks, sum_banks = banks[s]
            args = arg_pool.tile([P, 2, PAIR_TILES * HID], F32, tag="args")
            i_arg = args[:, 0, :]
            f_arg = args[:, 1, :]
            m_t = m_t_pool.tile([P, PAIR_TILES * HID], F32, tag="m_t")
            tile_cols = [slice(t * HID, (t + 1) * HID) for t in range(PAIR_TILES)]
            for t, cols in enumerate(tile_cols):
                nc.vector.tensor_tensor(out=i_arg[:, cols], in0=i_banks[t][:], in1=bi_all[:], op=ALU.add)
            for t, cols in enumerate(tile_cols):
                nc.vector.scalar_tensor_tensor(
                    out=m_t[:, cols], in0=sum_banks[t][:], scalar=-1.0, in1=i_arg[:, cols], op0=ALU.mult, op1=ALU.max
                )
            for t, cols in enumerate(tile_cols):
                nc.vector.scalar_tensor_tensor(
                    out=f_arg[:, cols], in0=sum_banks[t][:], scalar=-1.0, in1=m_t[:, cols], op0=ALU.mult, op1=ALU.subtract
                )
            nc.gpsimd.tensor_tensor(out=i_arg, in0=i_arg, in1=m_t[:], op=ALU.subtract)
            nc.sync.dma_start(out=pair_rows(out_0, s), in_=m_t[:])
            pair_args[s] = args

        def exponentials(s):
            both = pair_args[s][:].rearrange("p a w -> p (a w)")
            nc.scalar.activation(out=both, in_=both, func=ACT.Exp)
            nc.sync.dma_start(out=pair_rows(out_1, s), in_=pair_args[s][:, 0, :])
            nc.sync.dma_start(out=pair_rows(out_2, s), in_=pair_args[s][:, 1, :])

        bias_rows = consts.tile([P, P], BF16, tag="bias_rows")
        nc.vector.memset(bias_rows[:], 0.0)
        nc.scalar.dma_start(out=bias_rows[0:CHUNKS, :], in_=b_f.rearrange("(c p) -> c p", p=P))
        one = consts.tile([P, 1], F32, tag="one")
        nc.vector.memset(one[:], 1.0)
        warm = consts.tile([P, 1], F32, tag="warm")
        nc.scalar.activation(out=warm[:], in_=one[:], func=ACT.Exp)
        neg_ident = consts.tile([P, P], BF16, tag="neg_ident")
        nc.vector.tensor_scalar(out=neg_ident[:], in0=ident_bf16[:], scalar1=-1.0, scalar2=None, op0=ALU.mult)
        wfx_raw = load_weight(Wf_x)
        wfh_raw = load_weight(Wf_h)
        load_group_activations(0)

        bias_bank = psum.tile([P, P], BF16, tag="tr")
        nc.tensor.transpose(bias_bank[:], bias_rows[:], ident_bf16[:])
        neg_bf = consts.tile([P, CHUNKS], F32, tag="neg_bf")
        nc.vector.tensor_scalar(
            out=neg_bf[:], in0=bias_bank[:, 0:CHUNKS], scalar1=-1.0, scalar2=None, op0=ALU.mult
        )

        weights["fx"] = prepare_weight(wfx_raw, "wfx", "x", nc.scalar.copy)
        weights["fh"] = prepare_weight(wfh_raw, "wfh", "h", nc.scalar.copy)

        wix_raw = load_weight(Wi_x)
        load_group_activations(1)
        wih_raw = load_weight(Wi_h)
        bi_all = consts.tile([P, HID], BF16, tag="bi_all")
        nc.sync.dma_start(out=bi_all[:], in_=b_i.partition_broadcast(P))
        load_activations(1)
        load_m_prev(0)

        prepare_group(0, nc.scalar.copy)
        start_group(1, "ps")
        weights["ix"] = prepare_weight(wix_raw, "wix", "x", nc.vector.tensor_copy)
        forget_gate(0)
        middle_group(1, nc.vector.tensor_copy)
        finish_group(1, nc.vector.tensor_copy)
        start_group(2, "ps")
        weights["ih"] = prepare_weight(wih_raw, "wih", "h", nc.vector.tensor_copy)
        forget_gate(1)
        logarithms(0)
        load_activations(2)
        middle_group(2, nc.vector.tensor_copy)
        finish_group(2, nc.vector.tensor_copy)
        prepare_group(3, nc.vector.tensor_copy)
        load_activations(3)
        chain_banks(0)

        for k in range(N_ROUNDS):
            load_m_prev(k + 1)
            for g in round_groups(k + 1):
                forget_gate(g)
            logarithms(k + 1)
            round_pairs = range(k * ROUND_PAIRS, (k + 1) * ROUND_PAIRS)
            coming = round_groups(k + 2)
            last_round = k == N_ROUNDS - 1
            for s in round_pairs:
                chain(s)
                if s == round_pairs[-1] and coming:
                    start_group(coming[0], "tr")
                if s + 1 < N_PAIRS:
                    chain_banks(s + 1)
                if last_round:
                    exponentials(s)
            for g in coming:
                if g != coming[0]:
                    start_group(g, "tr")
                middle_group(g, nc.vector.tensor_copy)
                finish_group(g, nc.vector.tensor_copy)
            if not last_round:
                for s in round_pairs:
                    exponentials(s)
